import numpy as np
import ml_dtypes


def mxq(x, axis, fmt="e4m3"):
    dtype, down = {"e4m3": (ml_dtypes.float8_e4m3fn, 7), "e5m2": (ml_dtypes.float8_e5m2, 14)}[fmt]
    v = np.moveaxis(np.asarray(x, np.float32).astype(ml_dtypes.bfloat16).astype(np.float64), axis, -1)
    blocks = v.reshape(v.shape[:-1] + (-1, 32))
    amax = np.abs(blocks).max(-1, keepdims=True)
    byte = np.maximum(np.where(amax > 0, np.frexp(amax)[1] - 1 + 127, 0) - down, 1)
    scale = np.exp2(byte - 127.0)
    codes = (blocks / scale).astype(np.float32).astype(dtype).astype(np.float64)
    return np.moveaxis((codes * scale).reshape(v.shape), -1, axis)


WIDE = False


def mx_kscale(k):
    if not WIDE:
        return np.ones(k)
    levels = np.array([10, -10, 5, -5, 0])
    a = np.random.permutation(np.resize(levels, k // 512 * 4)).reshape(k // 512, 4)
    idx = np.arange(k)
    return np.exp2(a[idx // 512, idx % 128 // 32])


BF16 = ml_dtypes.bfloat16


def bf(x):
    return np.asarray(x, np.float32).astype(BF16)


def f64(x):
    return np.asarray(x).astype(np.float64)


E2M1 = np.array([0.0, 0.5, 1.0, 1.5, 2.0, 3.0, 4.0, 6.0, -0.0, -0.5, -1.0, -1.5, -2.0, -3.0, -4.0, -6.0])


def pack_weight(w, fmt):
    k, n = w.shape
    w = f64(bf(w)).reshape(k // 32, 32, n)
    amax = np.abs(w).max(1)
    if fmt == "e4m3":
        byte = np.frexp(amax)[1] - 1 + 127 - 7
    else:
        mant, ex = np.frexp(amax / 6.0)
        byte = np.where(mant > 0.5, ex, ex - 1) + 127
    byte = np.clip(np.where(amax > 0, byte, 1), 1, 254)
    scaled = (w * np.exp2(127.0 - byte)[:, None, :]).reshape(k, n).astype(np.float32)
    by_word = np.ascontiguousarray(scaled.reshape(k // 512, 128, 4, n).transpose(0, 1, 3, 2))
    if fmt == "e4m3":
        words = by_word.astype(ml_dtypes.float8_e4m3fn).view(np.uint8)
    else:
        c = by_word.astype(ml_dtypes.float4_e2m1fn).view(np.uint8) & 0xF
        words = c[..., 0::2] | (c[..., 1::2] << 4)
    return np.ascontiguousarray(words), np.ascontiguousarray(byte.astype(np.uint8).reshape(k // 512, 16, n))


def unpack_weight(words, scales, fmt):
    g, p, n, _ = words.shape
    if fmt == "e4m3":
        vals = np.ascontiguousarray(words).view(ml_dtypes.float8_e4m3fn).astype(np.float64)
    else:
        nib = np.empty((g, p, n, 4), np.uint8)
        nib[..., 0::2] = words & 0xF
        nib[..., 1::2] = words >> 4
        vals = E2M1[nib]
    vals = vals * np.repeat(np.exp2(scales.astype(np.float64) - 127.0), 8, axis=1)[..., None]
    return vals.transpose(0, 1, 3, 2).reshape(g * 512, n)


BS, N, D, B, D_PM = 2, 4096, 512, 8, 512


def setup_inputs():
    k, t = mx_kscale(D_PM), mx_kscale(D_PM)
    w = np.eye(D_PM) / B + 1.6 / np.sqrt(B * D_PM) * np.random.standard_normal((BS, B, D_PM, D_PM))
    pre = bf(np.random.standard_normal((BS, N, D_PM)) * k)
    W_pm = bf(w * t[:, None] / k)
    proj = np.random.standard_normal((D, D_PM)) / np.sqrt(D_PM) / t
    words, scales = pack_weight(proj.T, "e4m3")
    proj_out_b = bf(np.random.standard_normal(D) * 0.3)
    return {"pre": pre,
            "W_pm": W_pm,
            "proj_out_w_words": words,
            "proj_out_w_scales": scales,
            "proj_out_b": proj_out_b}


def reference(pre, W_pm, proj_out_w_words, proj_out_w_scales, proj_out_b):
    W_sum = np.sum(f64(W_pm), axis=1)
    post = mxq(f64(pre), 2, "e4m3") @ mxq(W_sum, 2, "e4m3").transpose(0, 2, 1)
    return (mxq(post, 2, "e4m3") @ unpack_weight(proj_out_w_words, proj_out_w_scales, "e4m3")) + f64(proj_out_b)

@@ -1,0 +1,263 @@
+from contextlib import ExitStack
+
+import concourse.mybir as mybir
+from concourse.masks import make_identity
+
+F32 = mybir.dt.float32
+BF16 = mybir.dt.bfloat16
+I32 = mybir.dt.int32
+U32 = mybir.dt.uint32
+U8 = mybir.dt.uint8
+FP8X4 = mybir.dt.float8_e4m3fn_x4
+ADD = mybir.AluOpType.add
+
+P = 128
+PACK = 4
+SAMPLES = 2
+TOKENS = 4096
+WIDTH = 512
+BANKS = 8
+VECTOR_BANKS = 2
+N_CHUNKS = SAMPLES * TOKENS // (PACK * P)
+N_TILES = N_CHUNKS * PACK
+
+TRANSPOSE_AHEAD = 4
+REGROUP_PRE_AHEAD = 3
+QUANTISE_PRE_AHEAD = 2
+FIRST_MATMUL_AHEAD = 6
+REGROUP_POST_AHEAD = 5
+QUANTISE_POST_AHEAD = 3
+SECOND_MATMUL_AHEAD = 2
+
+FLOPS = 2 * 2 * SAMPLES * TOKENS * WIDTH * WIDTH
+
+
+def tile_proceduralmemory_pc_t_kernel(
+    tc, pre, W_pm, proj_out_w_words, proj_out_w_scales, proj_out_b, out
+):
+    nc = tc.nc
+    pre_view = pre.rearrange("b (p s) i -> b p s i", p=P)
+    out_view = out.rearrange("b (p s) n -> b p s n", p=P)
+    mem_view = W_pm.rearrange("b k (p j) i -> b k p j i", j=PACK)
+
+    with ExitStack() as ctx:
+        ctx.enter_context(tc.manual_schedule())
+        const = ctx.enter_context(tc.tile_pool(name="const", bufs=1))
+        mem_pool = ctx.enter_context(tc.tile_pool(name="mem", bufs=BANKS))
+        pre_pool = ctx.enter_context(tc.tile_pool(name="pre", bufs=N_CHUNKS))
+        sum_pool = ctx.enter_context(tc.tile_pool(name="sum", bufs=2))
+        quarter_pool = ctx.enter_context(tc.tile_pool(name="quarter", bufs=PACK))
+        chunk_pool = ctx.enter_context(tc.tile_pool(name="chunk", bufs=3))
+        per_tile = ctx.enter_context(tc.tile_pool(name="per_tile", bufs=4))
+        store_pool = ctx.enter_context(tc.tile_pool(name="store", bufs=24))
+        tp_psum = ctx.enter_context(tc.psum_pool(name="tp", bufs=2))
+
+        ident_f32 = const.tile([P, P], F32)
+        make_identity(nc, ident_f32[:])
+        ident_bf = const.tile([P, P], BF16)
+        make_identity(nc, ident_bf[:])
+        ones = const.tile([P, P], BF16)
+        nc.vector.memset(ones[:], 1.0)
+        bias_rows = const.tile([P, WIDTH], BF16)
+        nc.vector.memset(bias_rows[:], 0.0)
+        w_scales = const.tile([P, WIDTH], U8, align_bytes=64)
+        nc.vector.memset(w_scales[:].bitcast(I32), 0)
+        w_codes = const.tile([P, WIDTH], U32, align_bytes=64)
+        bias_all = const.tile([P, WIDTH], F32)
+        mem_codes = [
+            const.tile([P, WIDTH], U32, align_bytes=64, name="mem_codes%d" % b) for b in range(SAMPLES)
+        ]
+        mem_scales = [
+            const.tile([P, WIDTH], U8, align_bytes=64, name="mem_scales%d" % b) for b in range(SAMPLES)
+        ]
+
+        def load_memory(b):
+            banks = []
+            for k in range(BANKS):
+                bank_sb = mem_pool.tile([P, PACK, WIDTH], BF16, name="bank_sb")
+                nc.sync.dma_start(out=bank_sb[:], in_=mem_view[b, k])
+                banks.append(bank_sb)
+            return banks
+
+        def load_chunk(g):
+            b, c = divmod(g, N_CHUNKS // SAMPLES)
+            pre_sb = pre_pool.tile([P, PACK, WIDTH], BF16, name="pre_sb")
+            nc.sync.dma_start(out=pre_sb[:], in_=pre_view[b, :, PACK * c : PACK * (c + 1), :])
+            return pre_sb
+
+        def load_projection():
+            nc.sync.dma_start(
+                out=w_codes[:].bitcast(I32),
+                in_=proj_out_w_words[0].rearrange("p n t -> p (n t)").bitcast(I32),
+            )
+            for q in range(4):
+                nc.sync.dma_start(
+                    out=w_scales[32 * q : 32 * q + 4, :].bitcast(I32),
+                    in_=proj_out_w_scales[0, 4 * q : 4 * q + 4, :].bitcast(I32),
+                )
+            nc.sync.dma_start(out=bias_rows[0:1, :], in_=proj_out_b.rearrange("(o n) -> o n", o=1))
+
+        def prepare_memory(b, banks, acc_psum):
+            pair = sum_pool.tile([P, PACK, WIDTH], F32, name="pair")
+            nc.vector.tensor_tensor(out=pair[:], in0=banks[0][:], in1=banks[1][:], op=ADD)
+            accs = [acc_psum.tile([P, WIDTH], F32, name="acc") for j in range(PACK)]
+            for k in range(VECTOR_BANKS, BANKS):
+                for j in range(PACK):
+                    nc.tensor.matmul(
+                        out=accs[j][:],
+                        lhsT=ident_bf[:],
+                        rhs=banks[k][:, j, :],
+                        start=(k == VECTOR_BANKS),
+                        stop=(k == BANKS - 1),
+                    )
+            grouped = []
+            for j in range(PACK):
+                w_sum = quarter_pool.tile([P, PACK, P], BF16, name="w_sum")
+                nc.vector.tensor_tensor(
+                    out=w_sum[:].rearrange("p (u e) q -> p u e q", u=2),
+                    in0=accs[j][:].rearrange("p (u q e) -> p u e q", u=2, e=2),
+                    in1=pair[:, j, :].rearrange("p (u q e) -> p u e q", u=2, e=2),
+                    op=ADD,
+                )
+                w_t = tp_psum.tile([P, PACK, P], BF16, name="tp_bank")
+                for t in range(PACK):
+                    nc.tensor.transpose(w_t[:, t, :], w_sum[:, t, :], ident_bf[:])
+                w_grouped = quarter_pool.tile([P, P, PACK], BF16, align_bytes=64, name="w_grouped")
+                nc.scalar.copy(out=w_grouped[:], in_=w_t[:].rearrange("q t c -> q c t"))
+                grouped.append(w_grouped)
+            for j in range(PACK):
+                cols = slice(j * P, (j + 1) * P)
+                nc.vector.quantize_mx(
+                    out=mem_codes[b][:, cols].bitcast(FP8X4),
+                    scales=mem_scales[b][:, cols],
+                    in_=grouped[j][:].rearrange("q c t -> q (c t)"),
+                )
+
+        def spread_bias():
+            bias_bank = tp_psum.tile([P, WIDTH], F32, name="tp_bank")
+            nc.tensor.matmul(out=bias_bank[:], lhsT=ones[:], rhs=bias_rows[:], start=True, stop=True)
+            nc.vector.tensor_copy(out=bias_all[:], in_=bias_bank[:])
+
+        pre_sb = {}
+        banks0 = load_memory(0)
+        with tc.psum_pool(name="acc", bufs=PACK) as acc_psum:
+            prepare_memory(0, banks0, acc_psum)
+            banks1 = load_memory(1)
+            pre_sb[0] = load_chunk(0)
+            load_projection()
+            for g in range(1, N_CHUNKS):
+                pre_sb[g] = load_chunk(g)
+            prepare_memory(1, banks1, acc_psum)
+        spread_bias()
+
+        post_psum = ctx.enter_context(tc.psum_pool(name="post", bufs=3, reuse_waits="tile"))
+        out_psum = ctx.enter_context(tc.psum_pool(name="outp", bufs=3, reuse_waits="tile"))
+
+        tp_banks, pre_grouped, pre_codes, pre_scales = {}, {}, {}, {}
+
+        def transpose_chunk(g):
+            if not 0 <= g < N_CHUNKS:
+                return
+            words = pre_sb[g][:].bitcast(F32)
+            for h in range(2):
+                tp_banks[g, h] = tp_psum.tile([P, 2, 2, P], F32, name="tp_bank")
+                for a in range(2):
+                    for u in range(2):
+                        nc.tensor.transpose(
+                            tp_banks[g, h][:, a, u, :],
+                            words[:, 2 * h + a, u * P : (u + 1) * P],
+                            ident_f32[:],
+                        )
+
+        def regroup_chunk(g):
+            if not 0 <= g < N_CHUNKS:
+                return
+            pre_grouped[g] = chunk_pool.tile([P, PACK, P, PACK], BF16, align_bytes=64, name="pre_grouped")
+            for h in range(2):
+                nc.scalar.copy(
+                    out=pre_grouped[g][:, 2 * h : 2 * h + 2, :, :].bitcast(F32),
+                    in_=tp_banks[g, h][:].rearrange("q a u c -> q a c u"),
+                )
+
+        def quantise_chunk(g):
+            if not 0 <= g < N_CHUNKS:
+                return
+            pre_codes[g] = chunk_pool.tile([P, PACK * P], U32, align_bytes=64, name="pre_codes")
+            pre_scales[g] = chunk_pool.tile([P, PACK * P], U8, align_bytes=64, name="pre_scales")
+            nc.vector.quantize_mx(
+                out=pre_codes[g][:].bitcast(FP8X4),
+                scales=pre_scales[g][:],
+                in_=pre_grouped[g][:].rearrange("q r c t -> q (r c t)"),
+            )
+
+        post_banks, post_grouped, post_codes, post_scales, out_banks = {}, {}, {}, {}, {}
+
+        def first_matmul(n):
+            if not 0 <= n < N_TILES:
+                return
+            g, r = divmod(n, PACK)
+            b = g // (N_CHUNKS // SAMPLES)
+            toks = slice(r * P, (r + 1) * P)
+            post_banks[n] = post_psum.tile([P, PACK, P], F32, name="post_bank")
+            for j in range(PACK):
+                cols = slice(j * P, (j + 1) * P)
+                nc.tensor.matmul_mx(
+                    out=post_banks[n][:, j, :],
+                    lhsT=mem_codes[b][:, cols].bitcast(FP8X4),
+                    lhsT_scale=mem_scales[b][:, cols],
+                    rhs=pre_codes[g][:, toks].bitcast(FP8X4),
+                    rhs_scale=pre_scales[g][:, toks],
+                    start=True,
+                    stop=True,
+                )
+
+        def regroup_post(n):
+            if not 0 <= n < N_TILES:
+                return
+            post_grouped[n] = per_tile.tile([P, P, PACK], BF16, align_bytes=64, name="post_grouped")
+            nc.scalar.copy(out=post_grouped[n][:], in_=post_banks[n][:].rearrange("p j c -> p c j"))
+
+        def quantise_post(n):
+            if not 0 <= n < N_TILES:
+                return
+            post_codes[n] = per_tile.tile([P, P], U32, align_bytes=64, name="post_codes")
+            post_scales[n] = per_tile.tile([P, P], U8, align_bytes=64, name="post_scales")
+            nc.vector.quantize_mx(
+                out=post_codes[n][:].bitcast(FP8X4),
+                scales=post_scales[n][:],
+                in_=post_grouped[n][:].rearrange("p c j -> p (c j)"),
+            )
+
+        def second_matmul(n):
+            if not 0 <= n < N_TILES:
+                return
+            out_banks[n] = out_psum.tile([P, WIDTH], F32, name="out_bank")
+            nc.tensor.matmul_mx(
+                out=out_banks[n][:],
+                lhsT=post_codes[n][:].bitcast(FP8X4),
+                lhsT_scale=post_scales[n][:],
+                rhs=w_codes[:].bitcast(FP8X4),
+                rhs_scale=w_scales[:],
+                start=True,
+                stop=True,
+            )
+
+        def add_bias_and_store(n):
+            if not 0 <= n < N_TILES:
+                return
+            b, s = divmod(n, N_TILES // SAMPLES)
+            out_sb = store_pool.tile([P, WIDTH], F32, name="out_sb")
+            nc.vector.tensor_tensor(out=out_sb[:], in0=out_banks[n][:], in1=bias_all[:], op=ADD)
+            nc.sync.dma_start(out=out_view[b, :, s, :], in_=out_sb[:])
+
+        for g in range(-TRANSPOSE_AHEAD, N_CHUNKS):
+            regroup_chunk(g + REGROUP_PRE_AHEAD)
+            transpose_chunk(g + TRANSPOSE_AHEAD)
+            quantise_chunk(g + QUANTISE_PRE_AHEAD)
+            for r in range(PACK):
+                n = PACK * g + r
+                second_matmul(n + SECOND_MATMUL_AHEAD)
+                first_matmul(n + FIRST_MATMUL_AHEAD)
+                regroup_post(n + REGROUP_POST_AHEAD)
+                add_bias_and_store(n)
+                quantise_post(n + QUANTISE_POST_AHEAD)

@@ -21,12 +21,13 @@ VECTOR_BANKS = 2
 N_CHUNKS = SAMPLES * TOKENS // (PACK * P)
 N_TILES = N_CHUNKS * PACK
 
-TRANSPOSE_AHEAD = 4
-REGROUP_PRE_AHEAD = 3
-QUANTISE_PRE_AHEAD = 2
-FIRST_MATMUL_AHEAD = 6
-REGROUP_POST_AHEAD = 5
-QUANTISE_POST_AHEAD = 3
+TRANSPOSE_AHEAD = 5
+REGROUP_PRE_AHEAD = 4
+QUANTISE_PRE_AHEAD = 3
+TRANSPOSE_BEFORE_TILE = 2
+FIRST_MATMUL_AHEAD = 7
+REGROUP_POST_AHEAD = 6
+QUANTISE_POST_AHEAD = 4
 SECOND_MATMUL_AHEAD = 2
 
 FLOPS = 2 * 2 * SAMPLES * TOKENS * WIDTH * WIDTH
@@ -47,10 +48,10 @@ def tile_proceduralmemory_pc_t_kernel(
         pre_pool = ctx.enter_context(tc.tile_pool(name="pre", bufs=N_CHUNKS))
         sum_pool = ctx.enter_context(tc.tile_pool(name="sum", bufs=2))
         quarter_pool = ctx.enter_context(tc.tile_pool(name="quarter", bufs=PACK))
-        chunk_pool = ctx.enter_context(tc.tile_pool(name="chunk", bufs=3))
-        per_tile = ctx.enter_context(tc.tile_pool(name="per_tile", bufs=4))
+        chunk_pool = ctx.enter_context(tc.tile_pool(name="chunk", bufs=4))
+        per_tile = ctx.enter_context(tc.tile_pool(name="per_tile", bufs=6))
         store_pool = ctx.enter_context(tc.tile_pool(name="store", bufs=24))
-        tp_psum = ctx.enter_context(tc.psum_pool(name="tp", bufs=2))
+        tp_psum = ctx.enter_context(tc.psum_pool(name="tp", bufs=3))
 
         ident_f32 = const.tile([P, P], F32)
         make_identity(nc, ident_f32[:])
@@ -151,7 +152,7 @@ def tile_proceduralmemory_pc_t_kernel(
         spread_bias()
 
         post_psum = ctx.enter_context(tc.psum_pool(name="post", bufs=3, reuse_waits="tile"))
-        out_psum = ctx.enter_context(tc.psum_pool(name="outp", bufs=3, reuse_waits="tile"))
+        out_psum = ctx.enter_context(tc.psum_pool(name="outp", bufs=2, reuse_waits="tile"))
 
         tp_banks, pre_grouped, pre_codes, pre_scales = {}, {}, {}, {}
 
@@ -252,10 +253,11 @@ def tile_proceduralmemory_pc_t_kernel(
 
         for g in range(-TRANSPOSE_AHEAD, N_CHUNKS):
             regroup_chunk(g + REGROUP_PRE_AHEAD)
-            transpose_chunk(g + TRANSPOSE_AHEAD)
             quantise_chunk(g + QUANTISE_PRE_AHEAD)
             for r in range(PACK):
                 n = PACK * g + r
+                if r == TRANSPOSE_BEFORE_TILE:
+                    transpose_chunk(g + TRANSPOSE_AHEAD)
                 second_matmul(n + SECOND_MATMUL_AHEAD)
                 first_matmul(n + FIRST_MATMUL_AHEAD)
                 regroup_post(n + REGROUP_POST_AHEAD)

@@ -20,14 +20,15 @@ BANKS = 8
 VECTOR_BANKS = 2
 N_CHUNKS = SAMPLES * TOKENS // (PACK * P)
 N_TILES = N_CHUNKS * PACK
+PAIR = 2
 
 TRANSPOSE_AHEAD = 5
 REGROUP_PRE_AHEAD = 4
 QUANTISE_PRE_AHEAD = 3
 TRANSPOSE_BEFORE_TILE = 2
-FIRST_MATMUL_AHEAD = 7
-REGROUP_POST_AHEAD = 6
-QUANTISE_POST_AHEAD = 4
+FIRST_MATMUL_AHEAD = 9
+REGROUP_POST_AHEAD = 8
+QUANTISE_POST_AHEAD = 5
 SECOND_MATMUL_AHEAD = 2
 
 FLOPS = 2 * 2 * SAMPLES * TOKENS * WIDTH * WIDTH
@@ -42,16 +43,15 @@ def tile_proceduralmemory_pc_t_kernel(
     mem_view = W_pm.rearrange("b k (p j) i -> b k p j i", j=PACK)
 
     with ExitStack() as ctx:
-        ctx.enter_context(tc.manual_schedule())
         const = ctx.enter_context(tc.tile_pool(name="const", bufs=1))
         mem_pool = ctx.enter_context(tc.tile_pool(name="mem", bufs=BANKS))
         pre_pool = ctx.enter_context(tc.tile_pool(name="pre", bufs=N_CHUNKS))
         sum_pool = ctx.enter_context(tc.tile_pool(name="sum", bufs=2))
         quarter_pool = ctx.enter_context(tc.tile_pool(name="quarter", bufs=PACK))
         chunk_pool = ctx.enter_context(tc.tile_pool(name="chunk", bufs=4))
-        per_tile = ctx.enter_context(tc.tile_pool(name="per_tile", bufs=6))
+        pair_pool = ctx.enter_context(tc.tile_pool(name="pair", bufs=4))
         store_pool = ctx.enter_context(tc.tile_pool(name="store", bufs=24))
-        tp_psum = ctx.enter_context(tc.psum_pool(name="tp", bufs=3))
+        tp_psum = ctx.enter_context(tc.psum_pool(name="tp", bufs=2))
 
         ident_f32 = const.tile([P, P], F32)
         make_identity(nc, ident_f32[:])
@@ -98,9 +98,11 @@ def tile_proceduralmemory_pc_t_kernel(
                 )
             nc.sync.dma_start(out=bias_rows[0:1, :], in_=proj_out_b.rearrange("(o n) -> o n", o=1))
 
-        def prepare_memory(b, banks, acc_psum):
-            pair = sum_pool.tile([P, PACK, WIDTH], F32, name="pair")
-            nc.vector.tensor_tensor(out=pair[:], in0=banks[0][:], in1=banks[1][:], op=ADD)
+        w_sum, w_t, w_grouped = {}, {}, {}
+
+        def sum_memory(b, banks, acc_psum):
+            pair_sum = sum_pool.tile([P, PACK, WIDTH], F32, name="pair_sum")
+            nc.vector.tensor_tensor(out=pair_sum[:], in0=banks[0][:], in1=banks[1][:], op=ADD)
             accs = [acc_psum.tile([P, WIDTH], F32, name="acc") for j in range(PACK)]
             for k in range(VECTOR_BANKS, BANKS):
                 for j in range(PACK):
@@ -111,28 +113,37 @@ def tile_proceduralmemory_pc_t_kernel(
                         start=(k == VECTOR_BANKS),
                         stop=(k == BANKS - 1),
                     )
-            grouped = []
             for j in range(PACK):
-                w_sum = quarter_pool.tile([P, PACK, P], BF16, name="w_sum")
+                w_sum[b, j] = quarter_pool.tile([P, PACK, P], BF16, name="w_sum")
                 nc.vector.tensor_tensor(
-                    out=w_sum[:].rearrange("p (u e) q -> p u e q", u=2),
+                    out=w_sum[b, j][:].rearrange("p (u e) q -> p u e q", u=2),
                     in0=accs[j][:].rearrange("p (u q e) -> p u e q", u=2, e=2),
-                    in1=pair[:, j, :].rearrange("p (u q e) -> p u e q", u=2, e=2),
+                    in1=pair_sum[:, j, :].rearrange("p (u q e) -> p u e q", u=2, e=2),
                     op=ADD,
                 )
-                w_t = tp_psum.tile([P, PACK, P], BF16, name="tp_bank")
-                for t in range(PACK):
-                    nc.tensor.transpose(w_t[:, t, :], w_sum[:, t, :], ident_bf[:])
-                w_grouped = quarter_pool.tile([P, P, PACK], BF16, align_bytes=64, name="w_grouped")
-                nc.scalar.copy(out=w_grouped[:], in_=w_t[:].rearrange("q t c -> q c t"))
-                grouped.append(w_grouped)
-            for j in range(PACK):
-                cols = slice(j * P, (j + 1) * P)
-                nc.vector.quantize_mx(
-                    out=mem_codes[b][:, cols].bitcast(FP8X4),
-                    scales=mem_scales[b][:, cols],
-                    in_=grouped[j][:].rearrange("q c t -> q (c t)"),
-                )
+
+        def transpose_quarter(b, j):
+            if not 0 <= j < PACK:
+                return
+            w_t[b, j] = tp_psum.tile([P, PACK, P], BF16, name="tp_bank")
+            for t in range(PACK):
+                nc.tensor.transpose(w_t[b, j][:, t, :], w_sum[b, j][:, t, :], ident_bf[:])
+
+        def regroup_quarter(b, j):
+            if not 0 <= j < PACK:
+                return
+            w_grouped[b, j] = quarter_pool.tile([P, P, PACK], BF16, align_bytes=64, name="w_grouped")
+            nc.scalar.copy(out=w_grouped[b, j][:], in_=w_t[b, j][:].rearrange("q t c -> q c t"))
+
+        def quantise_quarter(b, j):
+            if not 0 <= j < PACK:
+                return
+            cols = slice(j * P, (j + 1) * P)
+            nc.vector.quantize_mx(
+                out=mem_codes[b][:, cols].bitcast(FP8X4),
+                scales=mem_scales[b][:, cols],
+                in_=w_grouped[b, j][:].rearrange("q c t -> q (c t)"),
+            )
 
         def spread_bias():
             bias_bank = tp_psum.tile([P, WIDTH], F32, name="tp_bank")
@@ -142,17 +153,22 @@ def tile_proceduralmemory_pc_t_kernel(
         pre_sb = {}
         banks0 = load_memory(0)
         with tc.psum_pool(name="acc", bufs=PACK) as acc_psum:
-            prepare_memory(0, banks0, acc_psum)
+            sum_memory(0, banks0, acc_psum)
+            for j in range(PACK):
+                transpose_quarter(0, j)
+                regroup_quarter(0, j)
+            for j in range(PACK):
+                quantise_quarter(0, j)
             banks1 = load_memory(1)
             pre_sb[0] = load_chunk(0)
             load_projection()
             for g in range(1, N_CHUNKS):
                 pre_sb[g] = load_chunk(g)
-            prepare_memory(1, banks1, acc_psum)
+            sum_memory(1, banks1, acc_psum)
         spread_bias()
 
         post_psum = ctx.enter_context(tc.psum_pool(name="post", bufs=3, reuse_waits="tile"))
-        out_psum = ctx.enter_context(tc.psum_pool(name="outp", bufs=2, reuse_waits="tile"))
+        out_psum = ctx.enter_context(tc.psum_pool(name="outp", bufs=3, reuse_waits="tile"))
 
         tp_banks, pre_grouped, pre_codes, pre_scales = {}, {}, {}, {}
 
@@ -215,28 +231,35 @@ def tile_proceduralmemory_pc_t_kernel(
         def regroup_post(n):
             if not 0 <= n < N_TILES:
                 return
-            post_grouped[n] = per_tile.tile([P, P, PACK], BF16, align_bytes=64, name="post_grouped")
-            nc.scalar.copy(out=post_grouped[n][:], in_=post_banks[n][:].rearrange("p j c -> p c j"))
+            m, half = divmod(n, PAIR)
+            if half == 0:
+                post_grouped[m] = pair_pool.tile([P, PAIR, P, PACK], BF16, align_bytes=64, name="post_grouped")
+            nc.scalar.copy(
+                out=post_grouped[m][:, half, :, :], in_=post_banks[n][:].rearrange("p j c -> p c j")
+            )
 
         def quantise_post(n):
-            if not 0 <= n < N_TILES:
+            if not 0 <= n < N_TILES or n % PAIR != PAIR - 1:
                 return
-            post_codes[n] = per_tile.tile([P, P], U32, align_bytes=64, name="post_codes")
-            post_scales[n] = per_tile.tile([P, P], U8, align_bytes=64, name="post_scales")
+            m = n // PAIR
+            post_codes[m] = pair_pool.tile([P, PAIR * P], U32, align_bytes=64, name="post_codes")
+            post_scales[m] = pair_pool.tile([P, PAIR * P], U8, align_bytes=64, name="post_scales")
             nc.vector.quantize_mx(
-                out=post_codes[n][:].bitcast(FP8X4),
-                scales=post_scales[n][:],
-                in_=post_grouped[n][:].rearrange("p c j -> p (c j)"),
+                out=post_codes[m][:].bitcast(FP8X4),
+                scales=post_scales[m][:],
+                in_=post_grouped[m][:].rearrange("p h c j -> p (h c j)"),
             )
 
         def second_matmul(n):
             if not 0 <= n < N_TILES:
                 return
+            m, half = divmod(n, PAIR)
+            toks = slice(half * P, (half + 1) * P)
             out_banks[n] = out_psum.tile([P, WIDTH], F32, name="out_bank")
             nc.tensor.matmul_mx(
                 out=out_banks[n][:],
-                lhsT=post_codes[n][:].bitcast(FP8X4),
-                lhsT_scale=post_scales[n][:],
+                lhsT=post_codes[m][:, toks].bitcast(FP8X4),
+                lhsT_scale=post_scales[m][:, toks],
                 rhs=w_codes[:].bitcast(FP8X4),
                 rhs_scale=w_scales[:],
                 start=True,
@@ -253,11 +276,14 @@ def tile_proceduralmemory_pc_t_kernel(
 
         for g in range(-TRANSPOSE_AHEAD, N_CHUNKS):
             regroup_chunk(g + REGROUP_PRE_AHEAD)
+            regroup_quarter(1, g - 1)
+            quantise_quarter(1, g - 2)
             quantise_chunk(g + QUANTISE_PRE_AHEAD)
             for r in range(PACK):
                 n = PACK * g + r
                 if r == TRANSPOSE_BEFORE_TILE:
                     transpose_chunk(g + TRANSPOSE_AHEAD)
+                    transpose_quarter(1, g)
                 second_matmul(n + SECOND_MATMUL_AHEAD)
                 first_matmul(n + FIRST_MATMUL_AHEAD)
                 regroup_post(n + REGROUP_POST_AHEAD)

@@ -25,11 +25,11 @@ PAIR = 2
 TRANSPOSE_AHEAD = 5
 REGROUP_PRE_AHEAD = 4
 QUANTISE_PRE_AHEAD = 3
-TRANSPOSE_BEFORE_TILE = 2
+TRANSPOSE_BEFORE_TILE = 3
 FIRST_MATMUL_AHEAD = 9
 REGROUP_POST_AHEAD = 8
 QUANTISE_POST_AHEAD = 5
-SECOND_MATMUL_AHEAD = 2
+SECOND_MATMUL_AHEAD = 3
 
 FLOPS = 2 * 2 * SAMPLES * TOKENS * WIDTH * WIDTH
 
@@ -43,6 +43,7 @@ def tile_proceduralmemory_pc_t_kernel(
     mem_view = W_pm.rearrange("b k (p j) i -> b k p j i", j=PACK)
 
     with ExitStack() as ctx:
+        ctx.enter_context(tc.manual_schedule())
         const = ctx.enter_context(tc.tile_pool(name="const", bufs=1))
         mem_pool = ctx.enter_context(tc.tile_pool(name="mem", bufs=BANKS))
         pre_pool = ctx.enter_context(tc.tile_pool(name="pre", bufs=N_CHUNKS))
@@ -165,6 +166,11 @@ def tile_proceduralmemory_pc_t_kernel(
             for g in range(1, N_CHUNKS):
                 pre_sb[g] = load_chunk(g)
             sum_memory(1, banks1, acc_psum)
+            for j in range(PACK):
+                transpose_quarter(1, j)
+                regroup_quarter(1, j)
+            for j in range(PACK):
+                quantise_quarter(1, j)
         spread_bias()
 
         post_psum = ctx.enter_context(tc.psum_pool(name="post", bufs=3, reuse_waits="tile"))
@@ -276,14 +282,11 @@ def tile_proceduralmemory_pc_t_kernel(
 
         for g in range(-TRANSPOSE_AHEAD, N_CHUNKS):
             regroup_chunk(g + REGROUP_PRE_AHEAD)
-            regroup_quarter(1, g - 1)
-            quantise_quarter(1, g - 2)
             quantise_chunk(g + QUANTISE_PRE_AHEAD)
             for r in range(PACK):
                 n = PACK * g + r
                 if r == TRANSPOSE_BEFORE_TILE:
                     transpose_chunk(g + TRANSPOSE_AHEAD)
-                    transpose_quarter(1, g)
                 second_matmul(n + SECOND_MATMUL_AHEAD)
                 first_matmul(n + FIRST_MATMUL_AHEAD)
                 regroup_post(n + REGROUP_POST_AHEAD)

from contextlib import ExitStack

import concourse.mybir as mybir
from concourse.masks import make_identity

F32 = mybir.dt.float32
BF16 = mybir.dt.bfloat16
I32 = mybir.dt.int32
U32 = mybir.dt.uint32
U8 = mybir.dt.uint8
FP8X4 = mybir.dt.float8_e4m3fn_x4
ADD = mybir.AluOpType.add

P = 128
PACK = 4
SAMPLES = 2
TOKENS = 4096
WIDTH = 512
BANKS = 8
VECTOR_BANKS = 2
N_CHUNKS = SAMPLES * TOKENS // (PACK * P)
N_TILES = N_CHUNKS * PACK
PAIR = 2

TRANSPOSE_AHEAD = 5
REGROUP_PRE_AHEAD = 4
QUANTISE_PRE_AHEAD = 3
TRANSPOSE_BEFORE_TILE = 3
FIRST_MATMUL_AHEAD = 9
REGROUP_POST_AHEAD = 8
QUANTISE_POST_AHEAD = 5
SECOND_MATMUL_AHEAD = 3

FLOPS = 2 * 2 * SAMPLES * TOKENS * WIDTH * WIDTH


def tile_proceduralmemory_pc_t_kernel(
    tc, pre, W_pm, proj_out_w_words, proj_out_w_scales, proj_out_b, out
):
    nc = tc.nc
    pre_view = pre.rearrange("b (p s) i -> b p s i", p=P)
    out_view = out.rearrange("b (p s) n -> b p s n", p=P)
    mem_view = W_pm.rearrange("b k (p j) i -> b k p j i", j=PACK)

    with ExitStack() as ctx:
        ctx.enter_context(tc.manual_schedule())
        const = ctx.enter_context(tc.tile_pool(name="const", bufs=1))
        mem_pool = ctx.enter_context(tc.tile_pool(name="mem", bufs=BANKS))
        pre_pool = ctx.enter_context(tc.tile_pool(name="pre", bufs=N_CHUNKS))
        sum_pool = ctx.enter_context(tc.tile_pool(name="sum", bufs=2))
        quarter_pool = ctx.enter_context(tc.tile_pool(name="quarter", bufs=PACK))
        chunk_pool = ctx.enter_context(tc.tile_pool(name="chunk", bufs=4))
        pair_pool = ctx.enter_context(tc.tile_pool(name="pair", bufs=4))
        store_pool = ctx.enter_context(tc.tile_pool(name="store", bufs=24))
        tp_psum = ctx.enter_context(tc.psum_pool(name="tp", bufs=2))

        ident_f32 = const.tile([P, P], F32)
        make_identity(nc, ident_f32[:])
        ident_bf = const.tile([P, P], BF16)
        make_identity(nc, ident_bf[:])
        ones = const.tile([P, P], BF16)
        nc.vector.memset(ones[:], 1.0)
        bias_rows = const.tile([P, WIDTH], BF16)
        nc.vector.memset(bias_rows[:], 0.0)
        w_scales = const.tile([P, WIDTH], U8, align_bytes=64)
        nc.vector.memset(w_scales[:].bitcast(I32), 0)
        w_codes = const.tile([P, WIDTH], U32, align_bytes=64)
        bias_all = const.tile([P, WIDTH], F32)
        mem_codes = [
            const.tile([P, WIDTH], U32, align_bytes=64, name="mem_codes%d" % b) for b in range(SAMPLES)
        ]
        mem_scales = [
            const.tile([P, WIDTH], U8, align_bytes=64, name="mem_scales%d" % b) for b in range(SAMPLES)
        ]

        def load_memory(b):
            banks = []
            for k in range(BANKS):
                bank_sb = mem_pool.tile([P, PACK, WIDTH], BF16, name="bank_sb")
                nc.sync.dma_start(out=bank_sb[:], in_=mem_view[b, k])
                banks.append(bank_sb)
            return banks

        def load_chunk(g):
            b, c = divmod(g, N_CHUNKS // SAMPLES)
            pre_sb = pre_pool.tile([P, PACK, WIDTH], BF16, name="pre_sb")
            nc.sync.dma_start(out=pre_sb[:], in_=pre_view[b, :, PACK * c : PACK * (c + 1), :])
            return pre_sb

        def load_projection():
            nc.sync.dma_start(
                out=w_codes[:].bitcast(I32),
                in_=proj_out_w_words[0].rearrange("p n t -> p (n t)").bitcast(I32),
            )
            for q in range(4):
                nc.sync.dma_start(
                    out=w_scales[32 * q : 32 * q + 4, :].bitcast(I32),
                    in_=proj_out_w_scales[0, 4 * q : 4 * q + 4, :].bitcast(I32),
                )
            nc.sync.dma_start(out=bias_rows[0:1, :], in_=proj_out_b.rearrange("(o n) -> o n", o=1))

        w_sum, w_t, w_grouped = {}, {}, {}

        def sum_memory(b, banks, acc_psum):
            pair_sum = sum_pool.tile([P, PACK, WIDTH], F32, name="pair_sum")
            nc.vector.tensor_tensor(out=pair_sum[:], in0=banks[0][:], in1=banks[1][:], op=ADD)
            accs = [acc_psum.tile([P, WIDTH], F32, name="acc") for j in range(PACK)]
            for k in range(VECTOR_BANKS, BANKS):
                for j in range(PACK):
                    nc.tensor.matmul(
                        out=accs[j][:],
                        lhsT=ident_bf[:],
                        rhs=banks[k][:, j, :],
                        start=(k == VECTOR_BANKS),
                        stop=(k == BANKS - 1),
                    )
            for j in range(PACK):
                w_sum[b, j] = quarter_pool.tile([P, PACK, P], BF16, name="w_sum")
                nc.vector.tensor_tensor(
                    out=w_sum[b, j][:].rearrange("p (u e) q -> p u e q", u=2),
                    in0=accs[j][:].rearrange("p (u q e) -> p u e q", u=2, e=2),
                    in1=pair_sum[:, j, :].rearrange("p (u q e) -> p u e q", u=2, e=2),
                    op=ADD,
                )

        def transpose_quarter(b, j):
            if not 0 <= j < PACK:
                return
            w_t[b, j] = tp_psum.tile([P, PACK, P], BF16, name="tp_bank")
            for t in range(PACK):
                nc.tensor.transpose(w_t[b, j][:, t, :], w_sum[b, j][:, t, :], ident_bf[:])

        def regroup_quarter(b, j):
            if not 0 <= j < PACK:
                return
            w_grouped[b, j] = quarter_pool.tile([P, P, PACK], BF16, align_bytes=64, name="w_grouped")
            nc.scalar.copy(out=w_grouped[b, j][:], in_=w_t[b, j][:].rearrange("q t c -> q c t"))

        def quantise_quarter(b, j):
            if not 0 <= j < PACK:
                return
            cols = slice(j * P, (j + 1) * P)
            nc.vector.quantize_mx(
                out=mem_codes[b][:, cols].bitcast(FP8X4),
                scales=mem_scales[b][:, cols],
                in_=w_grouped[b, j][:].rearrange("q c t -> q (c t)"),
            )

        def spread_bias():
            bias_bank = tp_psum.tile([P, WIDTH], F32, name="tp_bank")
            nc.tensor.matmul(out=bias_bank[:], lhsT=ones[:], rhs=bias_rows[:], start=True, stop=True)
            nc.vector.tensor_copy(out=bias_all[:], in_=bias_bank[:])

        pre_sb = {}
        banks0 = load_memory(0)
        with tc.psum_pool(name="acc", bufs=PACK) as acc_psum:
            sum_memory(0, banks0, acc_psum)
            for j in range(PACK):
                transpose_quarter(0, j)
                regroup_quarter(0, j)
            for j in range(PACK):
                quantise_quarter(0, j)
            banks1 = load_memory(1)
            pre_sb[0] = load_chunk(0)
            load_projection()
            for g in range(1, N_CHUNKS):
                pre_sb[g] = load_chunk(g)
            sum_memory(1, banks1, acc_psum)
            for j in range(PACK):
                transpose_quarter(1, j)
                regroup_quarter(1, j)
            for j in range(PACK):
                quantise_quarter(1, j)
        spread_bias()

        post_psum = ctx.enter_context(tc.psum_pool(name="post", bufs=3, reuse_waits="tile"))
        out_psum = ctx.enter_context(tc.psum_pool(name="outp", bufs=3, reuse_waits="tile"))

        tp_banks, pre_grouped, pre_codes, pre_scales = {}, {}, {}, {}

        def transpose_chunk(g):
            if not 0 <= g < N_CHUNKS:
                return
            words = pre_sb[g][:].bitcast(F32)
            for h in range(2):
                tp_banks[g, h] = tp_psum.tile([P, 2, 2, P], F32, name="tp_bank")
                for a in range(2):
                    for u in range(2):
                        nc.tensor.transpose(
                            tp_banks[g, h][:, a, u, :],
                            words[:, 2 * h + a, u * P : (u + 1) * P],
                            ident_f32[:],
                        )

        def regroup_chunk(g):
            if not 0 <= g < N_CHUNKS:
                return
            pre_grouped[g] = chunk_pool.tile([P, PACK, P, PACK], BF16, align_bytes=64, name="pre_grouped")
            for h in range(2):
                nc.scalar.copy(
                    out=pre_grouped[g][:, 2 * h : 2 * h + 2, :, :].bitcast(F32),
                    in_=tp_banks[g, h][:].rearrange("q a u c -> q a c u"),
                )

        def quantise_chunk(g):
            if not 0 <= g < N_CHUNKS:
                return
            pre_codes[g] = chunk_pool.tile([P, PACK * P], U32, align_bytes=64, name="pre_codes")
            pre_scales[g] = chunk_pool.tile([P, PACK * P], U8, align_bytes=64, name="pre_scales")
            nc.vector.quantize_mx(
                out=pre_codes[g][:].bitcast(FP8X4),
                scales=pre_scales[g][:],
                in_=pre_grouped[g][:].rearrange("q r c t -> q (r c t)"),
            )

        post_banks, post_grouped, post_codes, post_scales, out_banks = {}, {}, {}, {}, {}

        def first_matmul(n):
            if not 0 <= n < N_TILES:
                return
            g, r = divmod(n, PACK)
            b = g // (N_CHUNKS // SAMPLES)
            toks = slice(r * P, (r + 1) * P)
            post_banks[n] = post_psum.tile([P, PACK, P], F32, name="post_bank")
            for j in range(PACK):
                cols = slice(j * P, (j + 1) * P)
                nc.tensor.matmul_mx(
                    out=post_banks[n][:, j, :],
                    lhsT=mem_codes[b][:, cols].bitcast(FP8X4),
                    lhsT_scale=mem_scales[b][:, cols],
                    rhs=pre_codes[g][:, toks].bitcast(FP8X4),
                    rhs_scale=pre_scales[g][:, toks],
                    start=True,
                    stop=True,
                )

        def regroup_post(n):
            if not 0 <= n < N_TILES:
                return
            m, half = divmod(n, PAIR)
            if half == 0:
                post_grouped[m] = pair_pool.tile([P, PAIR, P, PACK], BF16, align_bytes=64, name="post_grouped")
            nc.scalar.copy(
                out=post_grouped[m][:, half, :, :], in_=post_banks[n][:].rearrange("p j c -> p c j")
            )

        def quantise_post(n):
            if not 0 <= n < N_TILES or n % PAIR != PAIR - 1:
                return
            m = n // PAIR
            post_codes[m] = pair_pool.tile([P, PAIR * P], U32, align_bytes=64, name="post_codes")
            post_scales[m] = pair_pool.tile([P, PAIR * P], U8, align_bytes=64, name="post_scales")
            nc.vector.quantize_mx(
                out=post_codes[m][:].bitcast(FP8X4),
                scales=post_scales[m][:],
                in_=post_grouped[m][:].rearrange("p h c j -> p (h c j)"),
            )

        def second_matmul(n):
            if not 0 <= n < N_TILES:
                return
            m, half = divmod(n, PAIR)
            toks = slice(half * P, (half + 1) * P)
            out_banks[n] = out_psum.tile([P, WIDTH], F32, name="out_bank")
            nc.tensor.matmul_mx(
                out=out_banks[n][:],
                lhsT=post_codes[m][:, toks].bitcast(FP8X4),
                lhsT_scale=post_scales[m][:, toks],
                rhs=w_codes[:].bitcast(FP8X4),
                rhs_scale=w_scales[:],
                start=True,
                stop=True,
            )

        def add_bias_and_store(n):
            if not 0 <= n < N_TILES:
                return
            b, s = divmod(n, N_TILES // SAMPLES)
            out_sb = store_pool.tile([P, WIDTH], F32, name="out_sb")
            nc.vector.tensor_tensor(out=out_sb[:], in0=out_banks[n][:], in1=bias_all[:], op=ADD)
            nc.sync.dma_start(out=out_view[b, :, s, :], in_=out_sb[:])

        for g in range(-TRANSPOSE_AHEAD, N_CHUNKS):
            regroup_chunk(g + REGROUP_PRE_AHEAD)
            quantise_chunk(g + QUANTISE_PRE_AHEAD)
            for r in range(PACK):
                n = PACK * g + r
                if r == TRANSPOSE_BEFORE_TILE:
                    transpose_chunk(g + TRANSPOSE_AHEAD)
                second_matmul(n + SECOND_MATMUL_AHEAD)
                first_matmul(n + FIRST_MATMUL_AHEAD)
                regroup_post(n + REGROUP_POST_AHEAD)
                add_bias_and_store(n)
                quantise_post(n + QUANTISE_POST_AHEAD)
